import numpy as np
import ml_dtypes


def mxq(x, axis, fmt="e4m3"):
    dtype, down = {"e4m3": (ml_dtypes.float8_e4m3fn, 7), "e5m2": (ml_dtypes.float8_e5m2, 14)}[fmt]
    v = np.moveaxis(np.asarray(x, np.float32).astype(ml_dtypes.bfloat16).astype(np.float64), axis, -1)
    blocks = v.reshape(v.shape[:-1] + (-1, 32))
    amax = np.abs(blocks).max(-1, keepdims=True)
    byte = np.maximum(np.where(amax > 0, np.frexp(amax)[1] - 1 + 127, 0) - down, 1)
    scale = np.exp2(byte - 127.0)
    codes = (blocks / scale).astype(np.float32).astype(dtype).astype(np.float64)
    return np.moveaxis((codes * scale).reshape(v.shape), -1, axis)


WIDE = False


def mx_kscale(k):
    if not WIDE:
        return np.ones(k)
    levels = np.array([10, -10, 5, -5, 0])
    a = np.random.permutation(np.resize(levels, k // 512 * 4)).reshape(k // 512, 4)
    idx = np.arange(k)
    return np.exp2(a[idx // 512, idx % 128 // 32])


BF16 = ml_dtypes.bfloat16


def bf(x):
    return np.asarray(x, np.float32).astype(BF16)


def f64(x):
    return np.asarray(x).astype(np.float64)


B, Tq, Tk, C = 2, 512, 512, 1024
BETA = 2.35


def softplus(v):
    return np.log(1.0 + np.exp(v))


def setup_inputs():
    s = mx_kscale(C)
    level = np.random.standard_normal((B, Tk))[..., None]
    return {"q": bf(np.random.standard_normal((B, Tq, C)) * 1.5 * s),
            "k_mu": bf(np.random.standard_normal((B, Tk, C)) / s),
            "k_var": bf(softplus(np.random.standard_normal((B, Tk, C)) + level) / s / s),
            "v_sample": bf(np.random.standard_normal((B, Tk, C)) * 1.3)}


def reference(q, k_mu, k_var, v_sample):
    mean_scores = (mxq(f64(q), 2, "e4m3") @ mxq(f64(k_mu), 2, "e4m3").transpose(0, 2, 1)) / np.sqrt(C)
    q2 = f64(q) * f64(q)
    var_penalty = (mxq(q2, 2, "e4m3") @ mxq(f64(k_var), 2, "e4m3").transpose(0, 2, 1)) / C
    scores = mean_scores - BETA * np.sqrt(var_penalty)
    e = np.exp(scores - scores.max(-1, keepdims=True))
    return (mxq(e, 2, "e4m3") @ mxq(f64(v_sample), 1, "e4m3")) / e.sum(-1, keepdims=True)

@@ -1,0 +1,233 @@
+import math
+from contextlib import ExitStack
+
+import concourse.mybir as mybir
+from concourse.masks import make_identity
+
+F32 = mybir.dt.float32
+BF16 = mybir.dt.bfloat16
+U32 = mybir.dt.uint32
+U8 = mybir.dt.uint8
+FP8X4 = mybir.dt.float8_e4m3fn_x4
+ACT = mybir.ActivationFunctionType
+ALU = mybir.AluOpType
+AXIS = mybir.AxisListType
+
+P = 128
+PACK = 4
+BATCH, ROWS, CHANNELS = 2, 512, 1024
+BETA = 2.35
+ROW_TILES = ROWS // P
+PASSES = CHANNELS // (P * PACK)
+BANK = 512
+HALVES = CHANNELS // BANK
+
+FLOPS = 3 * 2 * BATCH * ROWS * ROWS * CHANNELS
+
+
+def tile_probcrossattention_pb_kernel(tc, q, k_mu, k_var, v_sample, out):
+    nc = tc.nc
+    with ExitStack() as ctx:
+        const = ctx.enter_context(tc.tile_pool(name="const", bufs=1))
+        raws = ctx.enter_context(tc.tile_pool(name="raws", bufs=1))
+        groups = ctx.enter_context(tc.tile_pool(name="groups", bufs=4))
+        packed = ctx.enter_context(tc.tile_pool(name="packed", bufs=1))
+        soft = ctx.enter_context(tc.tile_pool(name="soft", bufs=BATCH * ROW_TILES))
+        short = ctx.enter_context(tc.tile_pool(name="short", bufs=3))
+        psum_t = ctx.enter_context(tc.psum_pool(name="psum_t", bufs=4))
+        psum_mx = ctx.enter_context(tc.psum_pool(name="psum_mx", bufs=4))
+        ctx.enter_context(tc.manual_schedule())
+
+        def load(x, b, label):
+            raw = raws.tile([P, ROW_TILES * CHANNELS], BF16, name="raw_%s%d" % (label, b))
+            nc.sync.dma_start(out=raw[:], in_=x[b].rearrange("(p i) c -> p (i c)", i=ROW_TILES))
+            return raw
+
+        def new_group():
+            return groups.tile([P, ROWS * CHANNELS // P], BF16, name="group", align_bytes=64)
+
+        def transpose_row_tile(raw, i, group):
+            words = raw[:].bitcast(F32)
+            bank = psum_t.tile([P, BANK], F32, name="bank_t")
+            for w in range(BANK // P):
+                first = i * BANK + w * P
+                nc.tensor.transpose(bank[:, w * P : (w + 1) * P], words[:, first : first + P], ident_f32[:])
+            dst = group[:].bitcast(F32).rearrange("p (g r u) -> p g r u", g=PASSES, u=2)
+            nc.scalar.copy(
+                out=dst[:, :, i * P : (i + 1) * P, :],
+                in_=bank[:].rearrange("p (g u r) -> p g r u", g=PASSES, u=2),
+            )
+
+        def channels_to_partitions(raw):
+            group = new_group()
+            for i in range(ROW_TILES):
+                transpose_row_tile(raw, i, group)
+            return group
+
+        def quantise(group, label):
+            width = ROWS * CHANNELS // P // PACK
+            codes = packed.tile([P, width], U32, name="codes_" + label, align_bytes=64)
+            scales = packed.tile([P, width], U8, name="scales_" + label, align_bytes=64)
+            nc.vector.quantize_mx(out=codes[:].bitcast(FP8X4), scales=scales[:], in_=group[:])
+            return codes, scales
+
+        def square(group):
+            squared = new_group()
+            nc.vector.tensor_tensor(out=squared[:], in0=group[:], in1=group[:], op=ALU.mult)
+            return squared
+
+        def regroup_values(raw):
+            group = new_group()
+            for h in range(HALVES):
+                nc.vector.tensor_copy(
+                    out=group[:, h * BANK * PACK : (h + 1) * BANK * PACK].rearrange(
+                        "p (c i t) -> p c t i", i=4, t=PACK
+                    ),
+                    in_=raw[:].rearrange("p (t c) -> p t c", t=PACK)[:, :, h * BANK : (h + 1) * BANK].rearrange(
+                        "p t (c i) -> p c t i", i=4
+                    ),
+                )
+            return group
+
+        def channel_product(acc, rows_mx, keys_mx, i):
+            for g in range(PASSES):
+                rows = slice(g * ROWS + i * P, g * ROWS + (i + 1) * P)
+                keys = slice(g * ROWS, (g + 1) * ROWS)
+                nc.tensor.matmul_mx(
+                    out=acc[:],
+                    lhsT=rows_mx[0][:, rows].bitcast(FP8X4),
+                    lhsT_scale=rows_mx[1][:, rows],
+                    rhs=keys_mx[0][:, keys].bitcast(FP8X4),
+                    rhs_scale=keys_mx[1][:, keys],
+                    start=(g == 0),
+                    stop=(g == PASSES - 1),
+                )
+
+        def score_tile(b, i):
+            var_sum = psum_mx.tile([P, ROWS], F32, name="bank_mx")
+            channel_product(var_sum, qq_mx[b], k_var_mx[b], i)
+            mean_sum = psum_mx.tile([P, ROWS], F32, name="bank_mx")
+            channel_product(mean_sum, q_mx[b], k_mu_mx[b], i)
+            penalty = short.tile([P, ROWS], F32, name="penalty")
+            nc.scalar.activation(out=penalty[:], in_=var_sum[:], func=ACT.Sqrt, scale=BETA * BETA / CHANNELS)
+            neg_scores = soft.tile([P, ROWS], F32, name="neg_scores")
+            nc.vector.scalar_tensor_tensor(
+                out=neg_scores[:],
+                in0=mean_sum[:],
+                scalar=-1.0 / math.sqrt(CHANNELS),
+                in1=penalty[:],
+                op0=ALU.mult,
+                op1=ALU.add,
+            )
+            neg_max = soft.tile([P, 1], F32, name="neg_max")
+            nc.vector.tensor_reduce(out=neg_max[:], in_=neg_scores[:], axis=AXIS.X, op=ALU.min)
+            return neg_scores, neg_max
+
+        def exp_tile(neg_scores, neg_max):
+            e = soft.tile([P, ROWS], BF16, name="e")
+            row_sum = soft.tile([P, 1], F32, name="row_sum")
+            nc.scalar.activation(
+                out=e[:], in_=neg_scores[:], func=ACT.Exp, scale=-1.0, bias=neg_max[:], accum_out=row_sum[:]
+            )
+            return e, row_sum
+
+        def keys_to_partitions(e, row_sum, e_mx, i):
+            bank = psum_t.tile([P, ROWS], BF16, name="bank_t")
+            for t in range(PACK):
+                nc.tensor.transpose(bank[:, t * P : (t + 1) * P], e[:, t * P : (t + 1) * P], ident_bf16[:])
+            inv_sum = soft.tile([P, 1], F32, name="inv_sum")
+            nc.vector.reciprocal(out=inv_sum[:], in_=row_sum[:])
+            e_group = short.tile([P, ROWS], BF16, name="e_group", align_bytes=64)
+            nc.vector.tensor_copy(
+                out=e_group[:].rearrange("p (r t) -> p r t", t=PACK),
+                in_=bank[:].rearrange("p (t r) -> p r t", t=PACK),
+            )
+            rows = slice(i * P, (i + 1) * P)
+            nc.vector.quantize_mx(out=e_mx[0][:, rows].bitcast(FP8X4), scales=e_mx[1][:, rows], in_=e_group[:])
+            return inv_sum
+
+        def output_tile(b, i, e_mx, v_mx, inv_sum, second_half_on_vector):
+            rows = slice(i * P, (i + 1) * P)
+            result = short.tile([P, CHANNELS], F32, name="result")
+            for h in range(HALVES):
+                cols = slice(h * BANK, (h + 1) * BANK)
+                acc = psum_mx.tile([P, BANK], F32, name="bank_mx")
+                nc.tensor.matmul_mx(
+                    out=acc[:],
+                    lhsT=e_mx[0][:, rows].bitcast(FP8X4),
+                    lhsT_scale=e_mx[1][:, rows],
+                    rhs=v_mx[0][:, cols].bitcast(FP8X4),
+                    rhs_scale=v_mx[1][:, cols],
+                    start=True,
+                    stop=True,
+                )
+                if h == 1 and second_half_on_vector:
+                    nc.vector.tensor_scalar(
+                        out=result[:, cols], in0=acc[:], scalar1=inv_sum[:], scalar2=None, op0=ALU.mult
+                    )
+                else:
+                    nc.scalar.activation(out=result[:, cols], in_=acc[:], func=ACT.Copy, scale=inv_sum[:])
+            nc.sync.dma_start(
+                out=out[b].rearrange("(p i) c -> p i c", i=ROW_TILES)[:, i, :], in_=result[:]
+            )
+
+        raw_q, raw_k_mu, raw_k_var, raw_v = [], [], [], []
+        for b in range(BATCH):
+            raw_q.append(load(q, b, "q"))
+            raw_k_mu.append(load(k_mu, b, "k_mu"))
+            raw_k_var.append(load(k_var, b, "k_var"))
+        for b in range(BATCH):
+            raw_v.append(load(v_sample, b, "v"))
+
+        ident_f32 = const.tile([P, P], F32, name="ident_f32")
+        make_identity(nc, ident_f32[:])
+        ident_bf16 = const.tile([P, P], BF16, name="ident_bf16")
+        make_identity(nc, ident_bf16[:])
+        one = const.tile([P, 1], F32, name="one")
+        nc.vector.memset(one[:], 1.0)
+        nc.scalar.activation(out=one[:], in_=one[:], func=ACT.Sqrt)
+
+        q_mx, qq_mx, k_mu_mx, k_var_mx, v_mx, e_mx = [], [], [], [], [], []
+        for b in range(BATCH):
+            e_mx.append(
+                (
+                    packed.tile([P, ROWS], U32, name="codes_e%d" % b, align_bytes=64),
+                    packed.tile([P, ROWS], U8, name="scales_e%d" % b, align_bytes=64),
+                )
+            )
+
+        q_group = channels_to_partitions(raw_q[0])
+        q_mx.append(quantise(q_group, "q0"))
+        qq_group = square(q_group)
+        k_mu_group = channels_to_partitions(raw_k_mu[0])
+        k_mu_mx.append(quantise(k_mu_group, "k_mu0"))
+        qq_mx.append(quantise(qq_group, "qq0"))
+        k_var_group = channels_to_partitions(raw_k_var[0])
+        k_var_mx.append(quantise(k_var_group, "k_var0"))
+
+        q_group = channels_to_partitions(raw_q[1])
+        q_mx.append(quantise(q_group, "q1"))
+        qq_group = square(q_group)
+        scores = [[], []]
+        k_mu_group = new_group()
+        for i in range(ROW_TILES):
+            scores[0].append(score_tile(0, i))
+            transpose_row_tile(raw_k_mu[1], i, k_mu_group)
+        k_mu_mx.append(quantise(k_mu_group, "k_mu1"))
+        qq_mx.append(quantise(qq_group, "qq1"))
+        k_var_group = channels_to_partitions(raw_k_var[1])
+        k_var_mx.append(quantise(k_var_group, "k_var1"))
+
+        v_mx.append(quantise(regroup_values(raw_v[0]), "v0"))
+        for i in range(ROW_TILES):
+            scores[1].append(score_tile(1, i))
+
+        exps = [[exp_tile(*scores[0][i]) for i in range(ROW_TILES)]]
+        inv_sums = [[keys_to_partitions(*exps[0][i], e_mx[0], i) for i in range(ROW_TILES)]]
+        exps.append([exp_tile(*scores[1][i]) for i in range(ROW_TILES)])
+        v_mx.append(quantise(regroup_values(raw_v[1]), "v1"))
+        for i in range(ROW_TILES):
+            output_tile(0, i, e_mx[0], v_mx[0], inv_sums[0][i], False)
+        inv_sums.append([keys_to_partitions(*exps[1][i], e_mx[1], i) for i in range(ROW_TILES)])
+        for i in range(ROW_TILES):
+            output_tile(1, i, e_mx[1], v_mx[1], inv_sums[1][i], True)

@@ -21,6 +21,10 @@ ROW_TILES = ROWS // P
 PASSES = CHANNELS // (P * PACK)
 BANK = 512
 HALVES = CHANNELS // BANK
+OPERAND = ROWS * CHANNELS // P
+TILE_WORDS = OPERAND // PACK // ROW_TILES
+LOAD_PIECES = 2
+VALUE_PARTS = 4
 
 FLOPS = 3 * 2 * BATCH * ROWS * ROWS * CHANNELS
 
@@ -32,66 +36,82 @@ def tile_probcrossattention_pb_kernel(tc, q, k_mu, k_var, v_sample, out):
         raws = ctx.enter_context(tc.tile_pool(name="raws", bufs=1))
         groups = ctx.enter_context(tc.tile_pool(name="groups", bufs=4))
         packed = ctx.enter_context(tc.tile_pool(name="packed", bufs=1))
-        soft = ctx.enter_context(tc.tile_pool(name="soft", bufs=BATCH * ROW_TILES))
-        short = ctx.enter_context(tc.tile_pool(name="short", bufs=3))
-        psum_t = ctx.enter_context(tc.psum_pool(name="psum_t", bufs=4))
-        psum_mx = ctx.enter_context(tc.psum_pool(name="psum_mx", bufs=4))
+        penalties = ctx.enter_context(tc.tile_pool(name="penalties", bufs=BATCH * ROW_TILES))
+        stream = ctx.enter_context(tc.tile_pool(name="stream", bufs=4))
+        psum = ctx.enter_context(tc.psum_pool(name="psum", bufs=8))
         ctx.enter_context(tc.manual_schedule())
+
+        def bank(dtype):
+            return psum.tile([P, BANK], dtype, name="bank")
 
         def load(x, b, label):
             raw = raws.tile([P, ROW_TILES * CHANNELS], BF16, name="raw_%s%d" % (label, b))
-            nc.sync.dma_start(out=raw[:], in_=x[b].rearrange("(p i) c -> p (i c)", i=ROW_TILES))
+            rows = x[b].rearrange("(p i) c -> p (i c)", i=ROW_TILES)
+            piece = ROW_TILES * CHANNELS // LOAD_PIECES
+            for j in range(LOAD_PIECES):
+                nc.sync.dma_start(out=raw[:, j * piece : (j + 1) * piece], in_=rows[:, j * piece : (j + 1) * piece])
             return raw
 
         def new_group():
-            return groups.tile([P, ROWS * CHANNELS // P], BF16, name="group", align_bytes=64)
+            return groups.tile([P, OPERAND], BF16, name="group", align_bytes=64)
 
-        def transpose_row_tile(raw, i, group):
-            words = raw[:].bitcast(F32)
-            bank = psum_t.tile([P, BANK], F32, name="bank_t")
-            for w in range(BANK // P):
-                first = i * BANK + w * P
-                nc.tensor.transpose(bank[:, w * P : (w + 1) * P], words[:, first : first + P], ident_f32[:])
-            dst = group[:].bitcast(F32).rearrange("p (g r u) -> p g r u", g=PASSES, u=2)
-            nc.scalar.copy(
-                out=dst[:, :, i * P : (i + 1) * P, :],
-                in_=bank[:].rearrange("p (g u r) -> p g r u", g=PASSES, u=2),
+        def new_packed(label, width):
+            return (
+                packed.tile([P, width], U32, name="codes_" + label, align_bytes=64),
+                packed.tile([P, width], U8, name="scales_" + label, align_bytes=64),
             )
 
-        def channels_to_partitions(raw):
-            group = new_group()
+        def quantise(mx, group, first, width):
+            nc.vector.quantize_mx(
+                out=mx[0][:, first : first + width].bitcast(FP8X4),
+                scales=mx[1][:, first : first + width],
+                in_=group[:, first * PACK : (first + width) * PACK],
+            )
+
+        def transpose_row_tile(raw, i, group, order):
+            words = raw[:].bitcast(F32)
+            turned = bank(F32)
+            for w in range(BANK // P):
+                first = i * BANK + w * P
+                nc.tensor.transpose(turned[:, w * P : (w + 1) * P], words[:, first : first + P], ident_f32[:])
+            nc.scalar.copy(
+                out=group[:].bitcast(F32).rearrange(order, i=ROW_TILES, g=PASSES, u=2)[:, i],
+                in_=turned[:].rearrange("p (g u r) -> p g r u", g=PASSES, u=2),
+            )
+
+        def prepare_queries(b):
+            group, squared = new_group(), new_group()
+            q_mx.append(new_packed("q%d" % b, OPERAND // PACK))
             for i in range(ROW_TILES):
-                transpose_row_tile(raw, i, group)
-            return group
-
-        def quantise(group, label):
-            width = ROWS * CHANNELS // P // PACK
-            codes = packed.tile([P, width], U32, name="codes_" + label, align_bytes=64)
-            scales = packed.tile([P, width], U8, name="scales_" + label, align_bytes=64)
-            nc.vector.quantize_mx(out=codes[:].bitcast(FP8X4), scales=scales[:], in_=group[:])
-            return codes, scales
-
-        def square(group):
-            squared = new_group()
-            nc.vector.tensor_tensor(out=squared[:], in0=group[:], in1=group[:], op=ALU.mult)
+                transpose_row_tile(raw_q[b], i, group, "p (i g r u) -> p i g r u")
+                quantise(q_mx[b], group, i * TILE_WORDS, TILE_WORDS)
+                cols = slice(i * TILE_WORDS * PACK, (i + 1) * TILE_WORDS * PACK)
+                nc.vector.tensor_tensor(out=squared[:, cols], in0=group[:, cols], in1=group[:, cols], op=ALU.mult)
             return squared
 
-        def regroup_values(raw):
+        def prepare_keys(raw, label):
             group = new_group()
-            for h in range(HALVES):
-                nc.vector.tensor_copy(
-                    out=group[:, h * BANK * PACK : (h + 1) * BANK * PACK].rearrange(
-                        "p (c i t) -> p c t i", i=4, t=PACK
-                    ),
-                    in_=raw[:].rearrange("p (t c) -> p t c", t=PACK)[:, :, h * BANK : (h + 1) * BANK].rearrange(
-                        "p t (c i) -> p c t i", i=4
-                    ),
-                )
-            return group
+            for i in range(ROW_TILES):
+                transpose_row_tile(raw, i, group, "p (g i r u) -> p i g r u")
+            mx = new_packed(label, OPERAND // PACK)
+            quantise(mx, group, 0, OPERAND // PACK)
+            return mx
+
+        def prepare_values(b, group, part):
+            width = CHANNELS // VALUE_PARTS
+            nc.vector.tensor_copy(
+                out=group[:, part * width * PACK : (part + 1) * width * PACK].rearrange(
+                    "p (c i t) -> p c t i", i=4, t=PACK
+                ),
+                in_=raw_v[b][:]
+                .rearrange("p (t c) -> p t c", t=PACK)[:, :, part * width : (part + 1) * width]
+                .rearrange("p t (c i) -> p c t i", i=4),
+            )
+            quantise(v_mx[b], group, part * width, width)
 
         def channel_product(acc, rows_mx, keys_mx, i):
             for g in range(PASSES):
-                rows = slice(g * ROWS + i * P, g * ROWS + (i + 1) * P)
+                rows = slice((i * PASSES + g) * P, (i * PASSES + g + 1) * P)
                 keys = slice(g * ROWS, (g + 1) * ROWS)
                 nc.tensor.matmul_mx(
                     out=acc[:],
@@ -103,14 +123,17 @@ def tile_probcrossattention_pb_kernel(tc, q, k_mu, k_var, v_sample, out):
                     stop=(g == PASSES - 1),
                 )
 
-        def score_tile(b, i):
-            var_sum = psum_mx.tile([P, ROWS], F32, name="bank_mx")
+        def penalty_tile(b, i):
+            var_sum = bank(F32)
             channel_product(var_sum, qq_mx[b], k_var_mx[b], i)
-            mean_sum = psum_mx.tile([P, ROWS], F32, name="bank_mx")
-            channel_product(mean_sum, q_mx[b], k_mu_mx[b], i)
-            penalty = short.tile([P, ROWS], F32, name="penalty")
+            penalty = penalties.tile([P, ROWS], F32, name="penalty")
             nc.scalar.activation(out=penalty[:], in_=var_sum[:], func=ACT.Sqrt, scale=BETA * BETA / CHANNELS)
-            neg_scores = soft.tile([P, ROWS], F32, name="neg_scores")
+            return penalty
+
+        def score_tile(b, i, penalty):
+            mean_sum = bank(F32)
+            channel_product(mean_sum, q_mx[b], k_mu_mx[b], i)
+            neg_scores = stream.tile([P, ROWS], F32, name="neg_scores")
             nc.vector.scalar_tensor_tensor(
                 out=neg_scores[:],
                 in0=mean_sum[:],
@@ -119,57 +142,63 @@ def tile_probcrossattention_pb_kernel(tc, q, k_mu, k_var, v_sample, out):
                 op0=ALU.mult,
                 op1=ALU.add,
             )
-            neg_max = soft.tile([P, 1], F32, name="neg_max")
+            neg_max = stream.tile([P, 1], F32, name="neg_max")
             nc.vector.tensor_reduce(out=neg_max[:], in_=neg_scores[:], axis=AXIS.X, op=ALU.min)
             return neg_scores, neg_max
 
         def exp_tile(neg_scores, neg_max):
-            e = soft.tile([P, ROWS], BF16, name="e")
-            row_sum = soft.tile([P, 1], F32, name="row_sum")
+            e = stream.tile([P, ROWS], BF16, name="e")
+            row_sum = stream.tile([P, 1], F32, name="row_sum")
             nc.scalar.activation(
                 out=e[:], in_=neg_scores[:], func=ACT.Exp, scale=-1.0, bias=neg_max[:], accum_out=row_sum[:]
             )
-            return e, row_sum
-
-        def keys_to_partitions(e, row_sum, e_mx, i):
-            bank = psum_t.tile([P, ROWS], BF16, name="bank_t")
+            turned = bank(BF16)
             for t in range(PACK):
-                nc.tensor.transpose(bank[:, t * P : (t + 1) * P], e[:, t * P : (t + 1) * P], ident_bf16[:])
-            inv_sum = soft.tile([P, 1], F32, name="inv_sum")
-            nc.vector.reciprocal(out=inv_sum[:], in_=row_sum[:])
-            e_group = short.tile([P, ROWS], BF16, name="e_group", align_bytes=64)
-            nc.vector.tensor_copy(
-                out=e_group[:].rearrange("p (r t) -> p r t", t=PACK),
-                in_=bank[:].rearrange("p (t r) -> p r t", t=PACK),
-            )
-            rows = slice(i * P, (i + 1) * P)
-            nc.vector.quantize_mx(out=e_mx[0][:, rows].bitcast(FP8X4), scales=e_mx[1][:, rows], in_=e_group[:])
-            return inv_sum
+                nc.tensor.transpose(turned[:, t * P : (t + 1) * P], e[:, t * P : (t + 1) * P], ident_bf16[:])
+            return turned, row_sum
 
-        def output_tile(b, i, e_mx, v_mx, inv_sum, second_half_on_vector):
-            rows = slice(i * P, (i + 1) * P)
-            result = short.tile([P, CHANNELS], F32, name="result")
+        def pack_e_tile(turned, row_sum):
+            e_group = stream.tile([P, ROWS], BF16, name="e_group", align_bytes=64)
+            nc.scalar.copy(
+                out=e_group[:].rearrange("p (r t) -> p r t", t=PACK),
+                in_=turned[:].rearrange("p (t r) -> p r t", t=PACK),
+            )
+            inv_sum = stream.tile([P, 1], F32, name="inv_sum")
+            nc.vector.reciprocal(out=inv_sum[:], in_=row_sum[:])
+            e_mx = (
+                stream.tile([P, P], U32, name="codes_e", align_bytes=64),
+                stream.tile([P, P], U8, name="scales_e", align_bytes=64),
+            )
+            quantise(e_mx, e_group, 0, P)
+            return e_mx, inv_sum
+
+        def value_products(b, e_mx):
+            accs = []
             for h in range(HALVES):
                 cols = slice(h * BANK, (h + 1) * BANK)
-                acc = psum_mx.tile([P, BANK], F32, name="bank_mx")
+                acc = bank(F32)
                 nc.tensor.matmul_mx(
                     out=acc[:],
-                    lhsT=e_mx[0][:, rows].bitcast(FP8X4),
-                    lhsT_scale=e_mx[1][:, rows],
-                    rhs=v_mx[0][:, cols].bitcast(FP8X4),
-                    rhs_scale=v_mx[1][:, cols],
+                    lhsT=e_mx[0][:].bitcast(FP8X4),
+                    lhsT_scale=e_mx[1][:],
+                    rhs=v_mx[b][0][:, cols].bitcast(FP8X4),
+                    rhs_scale=v_mx[b][1][:, cols],
                     start=True,
                     stop=True,
                 )
-                if h == 1 and second_half_on_vector:
-                    nc.vector.tensor_scalar(
-                        out=result[:, cols], in0=acc[:], scalar1=inv_sum[:], scalar2=None, op0=ALU.mult
-                    )
-                else:
-                    nc.scalar.activation(out=result[:, cols], in_=acc[:], func=ACT.Copy, scale=inv_sum[:])
-            nc.sync.dma_start(
-                out=out[b].rearrange("(p i) c -> p i c", i=ROW_TILES)[:, i, :], in_=result[:]
-            )
+                accs.append(acc)
+            return accs
+
+        def store_tile(b, i, accs, inv_sum):
+            result = stream.tile([P, CHANNELS], F32, name="result")
+            nc.scalar.activation(out=result[:, 0:BANK], in_=accs[0][:], func=ACT.Copy, scale=inv_sum[:])
+            if b == 0:
+                nc.scalar.activation(out=result[:, BANK:], in_=accs[1][:], func=ACT.Copy, scale=inv_sum[:])
+            else:
+                nc.vector.tensor_scalar(
+                    out=result[:, BANK:], in0=accs[1][:], scalar1=inv_sum[:], scalar2=None, op0=ALU.mult
+                )
+            nc.sync.dma_start(out=out[b].rearrange("(p i) c -> p i c", i=ROW_TILES)[:, i, :], in_=result[:])
 
         raw_q, raw_k_mu, raw_k_var, raw_v = [], [], [], []
         for b in range(BATCH):
@@ -187,47 +216,32 @@ def tile_probcrossattention_pb_kernel(tc, q, k_mu, k_var, v_sample, out):
         nc.vector.memset(one[:], 1.0)
         nc.scalar.activation(out=one[:], in_=one[:], func=ACT.Sqrt)
 
-        q_mx, qq_mx, k_mu_mx, k_var_mx, v_mx, e_mx = [], [], [], [], [], []
+        q_mx, qq_mx, k_mu_mx, k_var_mx = [], [], [], []
         for b in range(BATCH):
-            e_mx.append(
-                (
-                    packed.tile([P, ROWS], U32, name="codes_e%d" % b, align_bytes=64),
-                    packed.tile([P, ROWS], U8, name="scales_e%d" % b, align_bytes=64),
-                )
-            )
+            squared = prepare_queries(b)
+            k_mu_mx.append(prepare_keys(raw_k_mu[b], "k_mu%d" % b))
+            qq_mx.append(new_packed("qq%d" % b, OPERAND // PACK))
+            quantise(qq_mx[b], squared, 0, OPERAND // PACK)
+            k_var_mx.append(prepare_keys(raw_k_var[b], "k_var%d" % b))
 
-        q_group = channels_to_partitions(raw_q[0])
-        q_mx.append(quantise(q_group, "q0"))
-        qq_group = square(q_group)
-        k_mu_group = channels_to_partitions(raw_k_mu[0])
-        k_mu_mx.append(quantise(k_mu_group, "k_mu0"))
-        qq_mx.append(quantise(qq_group, "qq0"))
-        k_var_group = channels_to_partitions(raw_k_var[0])
-        k_var_mx.append(quantise(k_var_group, "k_var0"))
+        tiles = [(b, i) for b in range(BATCH) for i in range(ROW_TILES)]
+        penalty_of = [penalty_tile(b, i) for (b, i) in tiles]
+        v_mx = [new_packed("v%d" % b, CHANNELS) for b in range(BATCH)]
+        v_group = [new_group() for b in range(BATCH)]
+        for part in range(VALUE_PARTS):
+            prepare_values(0, v_group[0], part)
 
-        q_group = channels_to_partitions(raw_q[1])
-        q_mx.append(quantise(q_group, "q1"))
-        qq_group = square(q_group)
-        scores = [[], []]
-        k_mu_group = new_group()
-        for i in range(ROW_TILES):
-            scores[0].append(score_tile(0, i))
-            transpose_row_tile(raw_k_mu[1], i, k_mu_group)
-        k_mu_mx.append(quantise(k_mu_group, "k_mu1"))
-        qq_mx.append(quantise(qq_group, "qq1"))
-        k_var_group = channels_to_partitions(raw_k_var[1])
-        k_var_mx.append(quantise(k_var_group, "k_var1"))
-
-        v_mx.append(quantise(regroup_values(raw_v[0]), "v0"))
-        for i in range(ROW_TILES):
-            scores[1].append(score_tile(1, i))
-
-        exps = [[exp_tile(*scores[0][i]) for i in range(ROW_TILES)]]
-        inv_sums = [[keys_to_partitions(*exps[0][i], e_mx[0], i) for i in range(ROW_TILES)]]
-        exps.append([exp_tile(*scores[1][i]) for i in range(ROW_TILES)])
-        v_mx.append(quantise(regroup_values(raw_v[1]), "v1"))
-        for i in range(ROW_TILES):
-            output_tile(0, i, e_mx[0], v_mx[0], inv_sums[0][i], False)
-        inv_sums.append([keys_to_partitions(*exps[1][i], e_mx[1], i) for i in range(ROW_TILES)])
-        for i in range(ROW_TILES):
-            output_tile(1, i, e_mx[1], v_mx[1], inv_sums[1][i], True)
+        scored, turned, packed_e, products = {}, {}, {}, {}
+        for step in range(len(tiles) + 3):
+            if step < len(tiles):
+                scored[step] = score_tile(*tiles[step], penalty_of[step])
+            if 0 <= step - 3 < len(tiles):
+                products[step - 3] = value_products(tiles[step - 3][0], packed_e[step - 3][0])
+            if 0 <= step - 1 < len(tiles):
+                turned[step - 1] = exp_tile(*scored[step - 1])
+            if 0 <= step - 2 < len(tiles):
+                packed_e[step - 2] = pack_e_tile(*turned[step - 2])
+            if 0 <= step - 3 < len(tiles):
+                store_tile(*tiles[step - 3], products[step - 3], packed_e[step - 3][1])
+            if 3 <= step < 3 + VALUE_PARTS:
+                prepare_values(1, v_group[1], step - 3)

@@ -22,9 +22,12 @@ PASSES = CHANNELS // (P * PACK)
 BANK = 512
 HALVES = CHANNELS // BANK
 OPERAND = ROWS * CHANNELS // P
-TILE_WORDS = OPERAND // PACK // ROW_TILES
+WORDS = OPERAND // PACK
 LOAD_PIECES = 2
 VALUE_PARTS = 4
+
+ROWS_STATIONARY = "p (i g r u) -> p i g r u"
+KEYS_MOVING = "p (g i r u) -> p i g r u"
 
 FLOPS = 3 * 2 * BATCH * ROWS * ROWS * CHANNELS
 
@@ -34,10 +37,10 @@ def tile_probcrossattention_pb_kernel(tc, q, k_mu, k_var, v_sample, out):
     with ExitStack() as ctx:
         const = ctx.enter_context(tc.tile_pool(name="const", bufs=1))
         raws = ctx.enter_context(tc.tile_pool(name="raws", bufs=1))
-        groups = ctx.enter_context(tc.tile_pool(name="groups", bufs=4))
+        groups = ctx.enter_context(tc.tile_pool(name="groups", bufs=5))
         packed = ctx.enter_context(tc.tile_pool(name="packed", bufs=1))
-        penalties = ctx.enter_context(tc.tile_pool(name="penalties", bufs=BATCH * ROW_TILES))
-        stream = ctx.enter_context(tc.tile_pool(name="stream", bufs=4))
+        per_tile = ctx.enter_context(tc.tile_pool(name="per_tile", bufs=BATCH * ROW_TILES))
+        per_batch = ctx.enter_context(tc.tile_pool(name="per_batch", bufs=ROW_TILES))
         psum = ctx.enter_context(tc.psum_pool(name="psum", bufs=8))
         ctx.enter_context(tc.manual_schedule())
 
@@ -45,9 +48,9 @@ def tile_probcrossattention_pb_kernel(tc, q, k_mu, k_var, v_sample, out):
             return psum.tile([P, BANK], dtype, name="bank")
 
         def load(x, b, label):
-            raw = raws.tile([P, ROW_TILES * CHANNELS], BF16, name="raw_%s%d" % (label, b))
+            raw = raws.tile([P, OPERAND], BF16, name="raw_%s%d" % (label, b))
             rows = x[b].rearrange("(p i) c -> p (i c)", i=ROW_TILES)
-            piece = ROW_TILES * CHANNELS // LOAD_PIECES
+            piece = OPERAND // LOAD_PIECES
             for j in range(LOAD_PIECES):
                 nc.sync.dma_start(out=raw[:, j * piece : (j + 1) * piece], in_=rows[:, j * piece : (j + 1) * piece])
             return raw
@@ -55,10 +58,10 @@ def tile_probcrossattention_pb_kernel(tc, q, k_mu, k_var, v_sample, out):
         def new_group():
             return groups.tile([P, OPERAND], BF16, name="group", align_bytes=64)
 
-        def new_packed(label, width):
+        def new_packed(pool, label, width):
             return (
-                packed.tile([P, width], U32, name="codes_" + label, align_bytes=64),
-                packed.tile([P, width], U8, name="scales_" + label, align_bytes=64),
+                pool.tile([P, width], U32, name="codes_" + label, align_bytes=64),
+                pool.tile([P, width], U8, name="scales_" + label, align_bytes=64),
             )
 
         def quantise(mx, group, first, width):
@@ -68,12 +71,20 @@ def tile_probcrossattention_pb_kernel(tc, q, k_mu, k_var, v_sample, out):
                 in_=group[:, first * PACK : (first + width) * PACK],
             )
 
-        def transpose_row_tile(raw, i, group, order):
+        def quantise_operand(group, label):
+            mx = new_packed(packed, label, WORDS)
+            quantise(mx, group, 0, WORDS)
+            return mx
+
+        def turn_row_tile(raw, i):
             words = raw[:].bitcast(F32)
             turned = bank(F32)
             for w in range(BANK // P):
                 first = i * BANK + w * P
                 nc.tensor.transpose(turned[:, w * P : (w + 1) * P], words[:, first : first + P], ident_f32[:])
+            return turned
+
+        def regroup_row_tile(turned, i, group, order):
             nc.scalar.copy(
                 out=group[:].bitcast(F32).rearrange(order, i=ROW_TILES, g=PASSES, u=2)[:, i],
                 in_=turned[:].rearrange("p (g u r) -> p g r u", g=PASSES, u=2),
@@ -81,23 +92,19 @@ def tile_probcrossattention_pb_kernel(tc, q, k_mu, k_var, v_sample, out):
 
         def prepare_queries(b):
             group, squared = new_group(), new_group()
-            q_mx.append(new_packed("q%d" % b, OPERAND // PACK))
             for i in range(ROW_TILES):
-                transpose_row_tile(raw_q[b], i, group, "p (i g r u) -> p i g r u")
-                quantise(q_mx[b], group, i * TILE_WORDS, TILE_WORDS)
-                cols = slice(i * TILE_WORDS * PACK, (i + 1) * TILE_WORDS * PACK)
+                regroup_row_tile(turn_row_tile(raw_q[b], i), i, group, ROWS_STATIONARY)
+                cols = slice(i * OPERAND // ROW_TILES, (i + 1) * OPERAND // ROW_TILES)
                 nc.vector.tensor_tensor(out=squared[:, cols], in0=group[:, cols], in1=group[:, cols], op=ALU.mult)
-            return squared
+            return group, squared
 
         def prepare_keys(raw, label):
             group = new_group()
             for i in range(ROW_TILES):
-                transpose_row_tile(raw, i, group, "p (g i r u) -> p i g r u")
-            mx = new_packed(label, OPERAND // PACK)
-            quantise(mx, group, 0, OPERAND // PACK)
-            return mx
+                regroup_row_tile(turn_row_tile(raw, i), i, group, KEYS_MOVING)
+            return quantise_operand(group, label)
 
-        def prepare_values(b, group, part):
+        def regroup_values(b, group, part):
             width = CHANNELS // VALUE_PARTS
             nc.vector.tensor_copy(
                 out=group[:, part * width * PACK : (part + 1) * width * PACK].rearrange(
@@ -107,9 +114,12 @@ def tile_probcrossattention_pb_kernel(tc, q, k_mu, k_var, v_sample, out):
                 .rearrange("p (t c) -> p t c", t=PACK)[:, :, part * width : (part + 1) * width]
                 .rearrange("p t (c i) -> p c t i", i=4),
             )
-            quantise(v_mx[b], group, part * width, width)
 
-        def channel_product(acc, rows_mx, keys_mx, i):
+        def quantise_values(b, group, part):
+            quantise(v_mx[b], group, part * CHANNELS // VALUE_PARTS, CHANNELS // VALUE_PARTS)
+
+        def channel_product(rows_mx, keys_mx, i):
+            acc = bank(F32)
             for g in range(PASSES):
                 rows = slice((i * PASSES + g) * P, (i * PASSES + g + 1) * P)
                 keys = slice(g * ROWS, (g + 1) * ROWS)
@@ -122,53 +132,58 @@ def tile_probcrossattention_pb_kernel(tc, q, k_mu, k_var, v_sample, out):
                     start=(g == 0),
                     stop=(g == PASSES - 1),
                 )
+            return acc
 
         def penalty_tile(b, i):
-            var_sum = bank(F32)
-            channel_product(var_sum, qq_mx[b], k_var_mx[b], i)
-            penalty = penalties.tile([P, ROWS], F32, name="penalty")
+            var_sum = channel_product(qq_mx[b], k_var_mx[b], i)
+            penalty = per_tile.tile([P, ROWS], F32, name="penalty")
             nc.scalar.activation(out=penalty[:], in_=var_sum[:], func=ACT.Sqrt, scale=BETA * BETA / CHANNELS)
             return penalty
 
-        def score_tile(b, i, penalty):
-            mean_sum = bank(F32)
-            channel_product(mean_sum, q_mx[b], k_mu_mx[b], i)
-            neg_scores = stream.tile([P, ROWS], F32, name="neg_scores")
-            nc.vector.scalar_tensor_tensor(
-                out=neg_scores[:],
-                in0=mean_sum[:],
-                scalar=-1.0 / math.sqrt(CHANNELS),
-                in1=penalty[:],
-                op0=ALU.mult,
-                op1=ALU.add,
-            )
-            neg_max = stream.tile([P, 1], F32, name="neg_max")
-            nc.vector.tensor_reduce(out=neg_max[:], in_=neg_scores[:], axis=AXIS.X, op=ALU.min)
+        def score_tiles(mean_sums, penalties):
+            neg_scores, neg_max = [], []
+            for i in range(ROW_TILES + 1):
+                if i < ROW_TILES:
+                    neg_scores.append(per_batch.tile([P, ROWS], F32, name="neg_scores"))
+                    nc.vector.scalar_tensor_tensor(
+                        out=neg_scores[i][:],
+                        in0=mean_sums[i][:],
+                        scalar=-1.0 / math.sqrt(CHANNELS),
+                        in1=penalties[i][:],
+                        op0=ALU.mult,
+                        op1=ALU.add,
+                    )
+                if i > 0:
+                    neg_max.append(per_batch.tile([P, 1], F32, name="neg_max"))
+                    nc.vector.tensor_reduce(out=neg_max[i - 1][:], in_=neg_scores[i - 1][:], axis=AXIS.X, op=ALU.min)
             return neg_scores, neg_max
 
         def exp_tile(neg_scores, neg_max):
-            e = stream.tile([P, ROWS], BF16, name="e")
-            row_sum = stream.tile([P, 1], F32, name="row_sum")
+            e = per_batch.tile([P, ROWS], BF16, name="e")
+            row_sum = per_batch.tile([P, 1], F32, name="row_sum")
             nc.scalar.activation(
                 out=e[:], in_=neg_scores[:], func=ACT.Exp, scale=-1.0, bias=neg_max[:], accum_out=row_sum[:]
             )
+            return e, row_sum
+
+        def turn_e(e):
             turned = bank(BF16)
             for t in range(PACK):
                 nc.tensor.transpose(turned[:, t * P : (t + 1) * P], e[:, t * P : (t + 1) * P], ident_bf16[:])
-            return turned, row_sum
+            return turned
 
-        def pack_e_tile(turned, row_sum):
-            e_group = stream.tile([P, ROWS], BF16, name="e_group", align_bytes=64)
+        def regroup_e(turned):
+            e_group = per_batch.tile([P, ROWS], BF16, name="e_group", align_bytes=64)
             nc.scalar.copy(
                 out=e_group[:].rearrange("p (r t) -> p r t", t=PACK),
                 in_=turned[:].rearrange("p (t r) -> p r t", t=PACK),
             )
-            inv_sum = stream.tile([P, 1], F32, name="inv_sum")
+            return e_group
+
+        def quantise_e(e_group, row_sum):
+            inv_sum = per_batch.tile([P, 1], F32, name="inv_sum")
             nc.vector.reciprocal(out=inv_sum[:], in_=row_sum[:])
-            e_mx = (
-                stream.tile([P, P], U32, name="codes_e", align_bytes=64),
-                stream.tile([P, P], U8, name="scales_e", align_bytes=64),
-            )
+            e_mx = new_packed(per_batch, "e", P)
             quantise(e_mx, e_group, 0, P)
             return e_mx, inv_sum
 
@@ -176,9 +191,9 @@ def tile_probcrossattention_pb_kernel(tc, q, k_mu, k_var, v_sample, out):
             accs = []
             for h in range(HALVES):
                 cols = slice(h * BANK, (h + 1) * BANK)
-                acc = bank(F32)
+                accs.append(bank(F32))
                 nc.tensor.matmul_mx(
-                    out=acc[:],
+                    out=accs[h][:],
                     lhsT=e_mx[0][:].bitcast(FP8X4),
                     lhsT_scale=e_mx[1][:],
                     rhs=v_mx[b][0][:, cols].bitcast(FP8X4),
@@ -186,11 +201,10 @@ def tile_probcrossattention_pb_kernel(tc, q, k_mu, k_var, v_sample, out):
                     start=True,
                     stop=True,
                 )
-                accs.append(acc)
             return accs
 
         def store_tile(b, i, accs, inv_sum):
-            result = stream.tile([P, CHANNELS], F32, name="result")
+            result = per_batch.tile([P, CHANNELS], F32, name="result")
             nc.scalar.activation(out=result[:, 0:BANK], in_=accs[0][:], func=ACT.Copy, scale=inv_sum[:])
             if b == 0:
                 nc.scalar.activation(out=result[:, BANK:], in_=accs[1][:], func=ACT.Copy, scale=inv_sum[:])
@@ -200,13 +214,15 @@ def tile_probcrossattention_pb_kernel(tc, q, k_mu, k_var, v_sample, out):
                 )
             nc.sync.dma_start(out=out[b].rearrange("(p i) c -> p i c", i=ROW_TILES)[:, i, :], in_=result[:])
 
-        raw_q, raw_k_mu, raw_k_var, raw_v = [], [], [], []
-        for b in range(BATCH):
-            raw_q.append(load(q, b, "q"))
-            raw_k_mu.append(load(k_mu, b, "k_mu"))
-            raw_k_var.append(load(k_var, b, "k_var"))
-        for b in range(BATCH):
-            raw_v.append(load(v_sample, b, "v"))
+        raw_q, raw_k_mu, raw_k_var, raw_v = {}, {}, {}, {}
+        raw_q[0] = load(q, 0, "q")
+        raw_k_var[0] = load(k_var, 0, "k_var")
+        raw_k_mu[0] = load(k_mu, 0, "k_mu")
+        raw_q[1] = load(q, 1, "q")
+        raw_k_var[1] = load(k_var, 1, "k_var")
+        raw_v[0] = load(v_sample, 0, "v")
+        raw_k_mu[1] = load(k_mu, 1, "k_mu")
+        raw_v[1] = load(v_sample, 1, "v")
 
         ident_f32 = const.tile([P, P], F32, name="ident_f32")
         make_identity(nc, ident_f32[:])
@@ -217,31 +233,55 @@ def tile_probcrossattention_pb_kernel(tc, q, k_mu, k_var, v_sample, out):
         nc.scalar.activation(out=one[:], in_=one[:], func=ACT.Sqrt)
 
         q_mx, qq_mx, k_mu_mx, k_var_mx = [], [], [], []
-        for b in range(BATCH):
-            squared = prepare_queries(b)
-            k_mu_mx.append(prepare_keys(raw_k_mu[b], "k_mu%d" % b))
-            qq_mx.append(new_packed("qq%d" % b, OPERAND // PACK))
-            quantise(qq_mx[b], squared, 0, OPERAND // PACK)
-            k_var_mx.append(prepare_keys(raw_k_var[b], "k_var%d" % b))
+        q_group, squared = prepare_queries(0)
+        q_mx.append(quantise_operand(q_group, "q0"))
+        qq_mx.append(quantise_operand(squared, "qq0"))
+        k_var_mx.append(prepare_keys(raw_k_var[0], "k_var0"))
+        k_mu_mx.append(prepare_keys(raw_k_mu[0], "k_mu0"))
+        q_group, squared = prepare_queries(1)
+        qq_mx.append(quantise_operand(squared, "qq1"))
+        k_var_mx.append(prepare_keys(raw_k_var[1], "k_var1"))
 
-        tiles = [(b, i) for b in range(BATCH) for i in range(ROW_TILES)]
-        penalty_of = [penalty_tile(b, i) for (b, i) in tiles]
-        v_mx = [new_packed("v%d" % b, CHANNELS) for b in range(BATCH)]
-        v_group = [new_group() for b in range(BATCH)]
-        for part in range(VALUE_PARTS):
-            prepare_values(0, v_group[0], part)
+        penalties = [[penalty_tile(b, i) for i in range(ROW_TILES)] for b in range(BATCH)]
+        v_mx = [new_packed(packed, "v%d" % b, CHANNELS) for b in range(BATCH)]
+        v_group = new_group()
+        for part in range(VALUE_PARTS + 1):
+            if part < VALUE_PARTS:
+                regroup_values(0, v_group, part)
+            if part > 0:
+                quantise_values(0, v_group, part - 1)
 
-        scored, turned, packed_e, products = {}, {}, {}, {}
-        for step in range(len(tiles) + 3):
-            if step < len(tiles):
-                scored[step] = score_tile(*tiles[step], penalty_of[step])
-            if 0 <= step - 3 < len(tiles):
-                products[step - 3] = value_products(tiles[step - 3][0], packed_e[step - 3][0])
-            if 0 <= step - 1 < len(tiles):
-                turned[step - 1] = exp_tile(*scored[step - 1])
-            if 0 <= step - 2 < len(tiles):
-                packed_e[step - 2] = pack_e_tile(*turned[step - 2])
-            if 0 <= step - 3 < len(tiles):
-                store_tile(*tiles[step - 3], products[step - 3], packed_e[step - 3][1])
-            if 3 <= step < 3 + VALUE_PARTS:
-                prepare_values(1, v_group[1], step - 3)
+        mean_sums = [channel_product(q_mx[0], k_mu_mx[0], i) for i in range(ROW_TILES)]
+        neg_scores, neg_max = score_tiles(mean_sums, penalties[0])
+        k_mu_turned = [turn_row_tile(raw_k_mu[1], i) for i in range(ROW_TILES)]
+        k_mu_group = new_group()
+        exps = []
+        for i in range(ROW_TILES):
+            exps.append(exp_tile(neg_scores[i], neg_max[i]))
+            regroup_row_tile(k_mu_turned[i], i, k_mu_group, KEYS_MOVING)
+        e_turned = [turn_e(exps[i][0]) for i in range(ROW_TILES)]
+        e_groups = [regroup_e(e_turned[i]) for i in range(ROW_TILES)]
+        q_mx.append(quantise_operand(q_group, "q1"))
+        v_group = new_group()
+        regroup_values(1, v_group, 0)
+        regroup_values(1, v_group, 1)
+        k_mu_mx.append(quantise_operand(k_mu_group, "k_mu1"))
+        e_mxs, products, mean_sums = [], [], []
+        for i in range(ROW_TILES):
+            e_mxs.append(quantise_e(e_groups[i], exps[i][1]))
+            quantise_values(1, v_group, i)
+            if i + 2 < VALUE_PARTS:
+                regroup_values(1, v_group, i + 2)
+            products.append(value_products(0, e_mxs[i][0]))
+            mean_sums.append(channel_product(q_mx[1], k_mu_mx[1], i))
+        neg_scores, neg_max = score_tiles(mean_sums, penalties[1])
+        for i in range(ROW_TILES):
+            store_tile(0, i, products[i], e_mxs[i][1])
+
+        exps = [exp_tile(neg_scores[i], neg_max[i]) for i in range(ROW_TILES)]
+        e_turned = [turn_e(exps[i][0]) for i in range(ROW_TILES)]
+        e_groups = [regroup_e(e_turned[i]) for i in range(ROW_TILES)]
+        e_mxs = [quantise_e(e_groups[i], exps[i][1]) for i in range(ROW_TILES)]
+        products = [value_products(1, e_mxs[i][0]) for i in range(ROW_TILES)]
+        for i in range(ROW_TILES):
+            store_tile(1, i, products[i], e_mxs[i][1])

@@ -25,6 +25,8 @@ OPERAND = ROWS * CHANNELS // P
 WORDS = OPERAND // PACK
 LOAD_PIECES = 2
 VALUE_PARTS = 4
+VALUES_FROM = 1
+SHARED_FROM = 3
 
 ROWS_STATIONARY = "p (i g r u) -> p i g r u"
 KEYS_MOVING = "p (g i r u) -> p i g r u"
@@ -40,7 +42,7 @@ def tile_probcrossattention_pb_kernel(tc, q, k_mu, k_var, v_sample, out):
         groups = ctx.enter_context(tc.tile_pool(name="groups", bufs=5))
         packed = ctx.enter_context(tc.tile_pool(name="packed", bufs=1))
         per_tile = ctx.enter_context(tc.tile_pool(name="per_tile", bufs=BATCH * ROW_TILES))
-        per_batch = ctx.enter_context(tc.tile_pool(name="per_batch", bufs=ROW_TILES))
+        stream = ctx.enter_context(tc.tile_pool(name="stream", bufs=4))
         psum = ctx.enter_context(tc.psum_pool(name="psum", bufs=8))
         ctx.enter_context(tc.manual_schedule())
 
@@ -140,29 +142,28 @@ def tile_probcrossattention_pb_kernel(tc, q, k_mu, k_var, v_sample, out):
             nc.scalar.activation(out=penalty[:], in_=var_sum[:], func=ACT.Sqrt, scale=BETA * BETA / CHANNELS)
             return penalty
 
-        def score_tiles(mean_sums, penalties):
-            neg_scores, neg_max = [], []
-            for i in range(ROW_TILES + 1):
-                if i < ROW_TILES:
-                    neg_scores.append(per_batch.tile([P, ROWS], F32, name="neg_scores"))
-                    nc.vector.scalar_tensor_tensor(
-                        out=neg_scores[i][:],
-                        in0=mean_sums[i][:],
-                        scalar=-1.0 / math.sqrt(CHANNELS),
-                        in1=penalties[i][:],
-                        op0=ALU.mult,
-                        op1=ALU.add,
-                    )
-                if i > 0:
-                    neg_max.append(per_batch.tile([P, 1], F32, name="neg_max"))
-                    nc.vector.tensor_reduce(out=neg_max[i - 1][:], in_=neg_scores[i - 1][:], axis=AXIS.X, op=ALU.min)
-            return neg_scores, neg_max
+        def negated_scores(mean_sum, penalty):
+            neg = stream.tile([P, ROWS], F32, name="neg")
+            nc.vector.scalar_tensor_tensor(
+                out=neg[:],
+                in0=mean_sum[:],
+                scalar=-1.0 / math.sqrt(CHANNELS),
+                in1=penalty[:],
+                op0=ALU.mult,
+                op1=ALU.add,
+            )
+            return neg
 
-        def exp_tile(neg_scores, neg_max):
-            e = per_batch.tile([P, ROWS], BF16, name="e")
-            row_sum = per_batch.tile([P, 1], F32, name="row_sum")
+        def row_minimum(neg):
+            low = stream.tile([P, 1], F32, name="low")
+            nc.vector.tensor_reduce(out=low[:], in_=neg[:], axis=AXIS.X, op=ALU.min)
+            return low
+
+        def exp_tile(neg, low):
+            e = stream.tile([P, ROWS], BF16, name="e")
+            row_sum = stream.tile([P, 1], F32, name="row_sum")
             nc.scalar.activation(
-                out=e[:], in_=neg_scores[:], func=ACT.Exp, scale=-1.0, bias=neg_max[:], accum_out=row_sum[:]
+                out=e[:], in_=neg[:], func=ACT.Exp, scale=-1.0, bias=low[:], accum_out=row_sum[:]
             )
             return e, row_sum
 
@@ -173,7 +174,7 @@ def tile_probcrossattention_pb_kernel(tc, q, k_mu, k_var, v_sample, out):
             return turned
 
         def regroup_e(turned):
-            e_group = per_batch.tile([P, ROWS], BF16, name="e_group", align_bytes=64)
+            e_group = stream.tile([P, ROWS], BF16, name="e_group", align_bytes=64)
             nc.scalar.copy(
                 out=e_group[:].rearrange("p (r t) -> p r t", t=PACK),
                 in_=turned[:].rearrange("p (t r) -> p r t", t=PACK),
@@ -181,9 +182,9 @@ def tile_probcrossattention_pb_kernel(tc, q, k_mu, k_var, v_sample, out):
             return e_group
 
         def quantise_e(e_group, row_sum):
-            inv_sum = per_batch.tile([P, 1], F32, name="inv_sum")
+            inv_sum = stream.tile([P, 1], F32, name="inv_sum")
             nc.vector.reciprocal(out=inv_sum[:], in_=row_sum[:])
-            e_mx = new_packed(per_batch, "e", P)
+            e_mx = new_packed(stream, "e", P)
             quantise(e_mx, e_group, 0, P)
             return e_mx, inv_sum
 
@@ -203,10 +204,11 @@ def tile_probcrossattention_pb_kernel(tc, q, k_mu, k_var, v_sample, out):
                 )
             return accs
 
-        def store_tile(b, i, accs, inv_sum):
-            result = per_batch.tile([P, CHANNELS], F32, name="result")
+        def store_tile(n, accs, inv_sum):
+            b, i = tiles[n]
+            result = stream.tile([P, CHANNELS], F32, name="result")
             nc.scalar.activation(out=result[:, 0:BANK], in_=accs[0][:], func=ACT.Copy, scale=inv_sum[:])
-            if b == 0:
+            if n < SHARED_FROM:
                 nc.scalar.activation(out=result[:, BANK:], in_=accs[1][:], func=ACT.Copy, scale=inv_sum[:])
             else:
                 nc.vector.tensor_scalar(
@@ -214,15 +216,13 @@ def tile_probcrossattention_pb_kernel(tc, q, k_mu, k_var, v_sample, out):
                 )
             nc.sync.dma_start(out=out[b].rearrange("(p i) c -> p i c", i=ROW_TILES)[:, i, :], in_=result[:])
 
-        raw_q, raw_k_mu, raw_k_var, raw_v = {}, {}, {}, {}
-        raw_q[0] = load(q, 0, "q")
-        raw_k_var[0] = load(k_var, 0, "k_var")
-        raw_k_mu[0] = load(k_mu, 0, "k_mu")
-        raw_q[1] = load(q, 1, "q")
-        raw_k_var[1] = load(k_var, 1, "k_var")
-        raw_v[0] = load(v_sample, 0, "v")
-        raw_k_mu[1] = load(k_mu, 1, "k_mu")
-        raw_v[1] = load(v_sample, 1, "v")
+        raw_q, raw_k_mu, raw_k_var, raw_v = [], [], [], []
+        for b in range(BATCH):
+            raw_q.append(load(q, b, "q"))
+            raw_k_var.append(load(k_var, b, "k_var"))
+            raw_k_mu.append(load(k_mu, b, "k_mu"))
+        for b in range(BATCH):
+            raw_v.append(load(v_sample, b, "v"))
 
         ident_f32 = const.tile([P, P], F32, name="ident_f32")
         make_identity(nc, ident_f32[:])
@@ -233,55 +233,47 @@ def tile_probcrossattention_pb_kernel(tc, q, k_mu, k_var, v_sample, out):
         nc.scalar.activation(out=one[:], in_=one[:], func=ACT.Sqrt)
 
         q_mx, qq_mx, k_mu_mx, k_var_mx = [], [], [], []
-        q_group, squared = prepare_queries(0)
-        q_mx.append(quantise_operand(q_group, "q0"))
-        qq_mx.append(quantise_operand(squared, "qq0"))
-        k_var_mx.append(prepare_keys(raw_k_var[0], "k_var0"))
-        k_mu_mx.append(prepare_keys(raw_k_mu[0], "k_mu0"))
-        q_group, squared = prepare_queries(1)
-        qq_mx.append(quantise_operand(squared, "qq1"))
-        k_var_mx.append(prepare_keys(raw_k_var[1], "k_var1"))
+        for b in range(BATCH):
+            q_group, squared = prepare_queries(b)
+            q_mx.append(quantise_operand(q_group, "q%d" % b))
+            qq_mx.append(quantise_operand(squared, "qq%d" % b))
+            k_var_mx.append(prepare_keys(raw_k_var[b], "k_var%d" % b))
+            k_mu_mx.append(prepare_keys(raw_k_mu[b], "k_mu%d" % b))
 
-        penalties = [[penalty_tile(b, i) for i in range(ROW_TILES)] for b in range(BATCH)]
+        tiles = [(b, i) for b in range(BATCH) for i in range(ROW_TILES)]
+        penalties = [penalty_tile(b, i) for (b, i) in tiles]
         v_mx = [new_packed(packed, "v%d" % b, CHANNELS) for b in range(BATCH)]
-        v_group = new_group()
+        v_groups = [new_group() for b in range(BATCH)]
         for part in range(VALUE_PARTS + 1):
             if part < VALUE_PARTS:
-                regroup_values(0, v_group, part)
+                regroup_values(0, v_groups[0], part)
             if part > 0:
-                quantise_values(0, v_group, part - 1)
+                quantise_values(0, v_groups[0], part - 1)
 
-        mean_sums = [channel_product(q_mx[0], k_mu_mx[0], i) for i in range(ROW_TILES)]
-        neg_scores, neg_max = score_tiles(mean_sums, penalties[0])
-        k_mu_turned = [turn_row_tile(raw_k_mu[1], i) for i in range(ROW_TILES)]
-        k_mu_group = new_group()
-        exps = []
-        for i in range(ROW_TILES):
-            exps.append(exp_tile(neg_scores[i], neg_max[i]))
-            regroup_row_tile(k_mu_turned[i], i, k_mu_group, KEYS_MOVING)
-        e_turned = [turn_e(exps[i][0]) for i in range(ROW_TILES)]
-        e_groups = [regroup_e(e_turned[i]) for i in range(ROW_TILES)]
-        q_mx.append(quantise_operand(q_group, "q1"))
-        v_group = new_group()
-        regroup_values(1, v_group, 0)
-        regroup_values(1, v_group, 1)
-        k_mu_mx.append(quantise_operand(k_mu_group, "k_mu1"))
-        e_mxs, products, mean_sums = [], [], []
-        for i in range(ROW_TILES):
-            e_mxs.append(quantise_e(e_groups[i], exps[i][1]))
-            quantise_values(1, v_group, i)
-            if i + 2 < VALUE_PARTS:
-                regroup_values(1, v_group, i + 2)
-            products.append(value_products(0, e_mxs[i][0]))
-            mean_sums.append(channel_product(q_mx[1], k_mu_mx[1], i))
-        neg_scores, neg_max = score_tiles(mean_sums, penalties[1])
-        for i in range(ROW_TILES):
-            store_tile(0, i, products[i], e_mxs[i][1])
+        def live(n):
+            return 0 <= n < len(tiles)
 
-        exps = [exp_tile(neg_scores[i], neg_max[i]) for i in range(ROW_TILES)]
-        e_turned = [turn_e(exps[i][0]) for i in range(ROW_TILES)]
-        e_groups = [regroup_e(e_turned[i]) for i in range(ROW_TILES)]
-        e_mxs = [quantise_e(e_groups[i], exps[i][1]) for i in range(ROW_TILES)]
-        products = [value_products(1, e_mxs[i][0]) for i in range(ROW_TILES)]
-        for i in range(ROW_TILES):
-            store_tile(1, i, products[i], e_mxs[i][1])
+        mean_sums, negs, lows, exps, e_turned, e_groups, e_mxs, products = {}, {}, {}, {}, {}, {}, {}, {}
+        for step in range(-3, len(tiles) + 3):
+            if live(step + 3):
+                b, i = tiles[step + 3]
+                mean_sums[step + 3] = channel_product(q_mx[b], k_mu_mx[b], i)
+            if live(step - 2):
+                products[step - 2] = value_products(tiles[step - 2][0], e_mxs[step - 2][0])
+            if live(step):
+                exps[step] = exp_tile(negs[step], lows[step])
+                e_turned[step] = turn_e(exps[step][0])
+            if live(step - 1):
+                e_groups[step - 1] = regroup_e(e_turned[step - 1])
+            if live(step + 2):
+                negs[step + 2] = negated_scores(mean_sums[step + 2], penalties[step + 2])
+            if live(step + 1):
+                lows[step + 1] = row_minimum(negs[step + 1])
+            if live(step - 3):
+                store_tile(step - 3, products[step - 3], e_mxs[step - 3][1])
+            if 0 <= step - VALUES_FROM < VALUE_PARTS:
+                regroup_values(1, v_groups[1], step - VALUES_FROM)
+            if live(step - 1):
+                e_mxs[step - 1] = quantise_e(e_groups[step - 1], exps[step - 1][1])
+            if 0 <= step - VALUES_FROM - 1 < VALUE_PARTS:
+                quantise_values(1, v_groups[1], step - VALUES_FROM - 1)

@@ -29,7 +29,6 @@ VALUES_FROM = 1
 SHARED_FROM = 3
 
 ROWS_STATIONARY = "p (i g r u) -> p i g r u"
-KEYS_MOVING = "p (g i r u) -> p i g r u"
 
 FLOPS = 3 * 2 * BATCH * ROWS * ROWS * CHANNELS
 
@@ -86,24 +85,40 @@ def tile_probcrossattention_pb_kernel(tc, q, k_mu, k_var, v_sample, out):
                 nc.tensor.transpose(turned[:, w * P : (w + 1) * P], words[:, first : first + P], ident_f32[:])
             return turned
 
-        def regroup_row_tile(turned, i, group, order):
+        def regroup_row_tile(turned, i, group):
             nc.scalar.copy(
-                out=group[:].bitcast(F32).rearrange(order, i=ROW_TILES, g=PASSES, u=2)[:, i],
+                out=group[:].bitcast(F32).rearrange(ROWS_STATIONARY, i=ROW_TILES, g=PASSES, u=2)[:, i],
                 in_=turned[:].rearrange("p (g u r) -> p g r u", g=PASSES, u=2),
             )
 
         def prepare_queries(b):
             group, squared = new_group(), new_group()
             for i in range(ROW_TILES):
-                regroup_row_tile(turn_row_tile(raw_q[b], i), i, group, ROWS_STATIONARY)
+                regroup_row_tile(turn_row_tile(raw_q[b], i), i, group)
                 cols = slice(i * OPERAND // ROW_TILES, (i + 1) * OPERAND // ROW_TILES)
                 nc.vector.tensor_tensor(out=squared[:, cols], in0=group[:, cols], in1=group[:, cols], op=ALU.mult)
             return group, squared
 
+        def turn_key_pair(raw, pair, g):
+            words = raw[:].bitcast(F32)
+            turned = bank(F32)
+            for x in range(BANK // P):
+                first = (2 * pair + x // 2) * BANK + (2 * g + x % 2) * P
+                nc.tensor.transpose(turned[:, x * P : (x + 1) * P], words[:, first : first + P], ident_f32[:])
+            return turned
+
+        def regroup_key_pair(turned, pair, g, group):
+            first = (g * 2 + pair) * BANK
+            nc.scalar.copy(
+                out=group[:].bitcast(F32)[:, first : first + BANK].rearrange("p (r x) -> p r x", x=4),
+                in_=turned[:].rearrange("p (x r) -> p r x", x=4),
+            )
+
         def prepare_keys(raw, label):
             group = new_group()
-            for i in range(ROW_TILES):
-                regroup_row_tile(turn_row_tile(raw, i), i, group, KEYS_MOVING)
+            for pair in range(ROW_TILES // 2):
+                for g in range(PASSES):
+                    regroup_key_pair(turn_key_pair(raw, pair, g), pair, g, group)
             return quantise_operand(group, label)
 
         def regroup_values(b, group, part):
@@ -168,16 +183,17 @@ def tile_probcrossattention_pb_kernel(tc, q, k_mu, k_var, v_sample, out):
             return e, row_sum
 
         def turn_e(e):
-            turned = bank(BF16)
-            for t in range(PACK):
-                nc.tensor.transpose(turned[:, t * P : (t + 1) * P], e[:, t * P : (t + 1) * P], ident_bf16[:])
+            words = e[:].bitcast(F32)
+            turned = bank(F32)
+            for u in range(2):
+                nc.tensor.transpose(turned[:, u * P : (u + 1) * P], words[:, u * P : (u + 1) * P], ident_f32[:])
             return turned
 
         def regroup_e(turned):
             e_group = stream.tile([P, ROWS], BF16, name="e_group", align_bytes=64)
             nc.scalar.copy(
-                out=e_group[:].rearrange("p (r t) -> p r t", t=PACK),
-                in_=turned[:].rearrange("p (t r) -> p r t", t=PACK),
+                out=e_group[:].bitcast(F32).rearrange("p (r u) -> p r u", u=2),
+                in_=turned[:, 0 : 2 * P].rearrange("p (u r) -> p r u", u=2),
             )
             return e_group
 
@@ -226,8 +242,6 @@ def tile_probcrossattention_pb_kernel(tc, q, k_mu, k_var, v_sample, out):
 
         ident_f32 = const.tile([P, P], F32, name="ident_f32")
         make_identity(nc, ident_f32[:])
-        ident_bf16 = const.tile([P, P], BF16, name="ident_bf16")
-        make_identity(nc, ident_bf16[:])
         one = const.tile([P, 1], F32, name="one")
         nc.vector.memset(one[:], 1.0)
         nc.scalar.activation(out=one[:], in_=one[:], func=ACT.Sqrt)

@@ -24,6 +24,7 @@ HALVES = CHANNELS // BANK
 OPERAND = ROWS * CHANNELS // P
 WORDS = OPERAND // PACK
 LOAD_PIECES = 2
+WARM_UP = 4
 VALUE_PARTS = 4
 VALUES_FROM = 1
 SHARED_FROM = 3
@@ -42,11 +43,16 @@ def tile_probcrossattention_pb_kernel(tc, q, k_mu, k_var, v_sample, out):
         packed = ctx.enter_context(tc.tile_pool(name="packed", bufs=1))
         per_tile = ctx.enter_context(tc.tile_pool(name="per_tile", bufs=BATCH * ROW_TILES))
         stream = ctx.enter_context(tc.tile_pool(name="stream", bufs=4))
-        psum = ctx.enter_context(tc.psum_pool(name="psum", bufs=8))
+        psum = ctx.enter_context(tc.psum_pool(name="psum", bufs=7))
+        spare = ctx.enter_context(tc.psum_pool(name="spare", bufs=1))
         ctx.enter_context(tc.manual_schedule())
 
         def bank(dtype):
             return psum.tile([P, BANK], dtype, name="bank")
+
+        def keep_warm(count):
+            for j in range(count):
+                nc.tensor.matmul(unread[:], idle[:, 0:P], idle[:], start=True, stop=True)
 
         def load(x, b, label):
             raw = raws.tile([P, OPERAND], BF16, name="raw_%s%d" % (label, b))
@@ -97,6 +103,8 @@ def tile_probcrossattention_pb_kernel(tc, q, k_mu, k_var, v_sample, out):
                 regroup_row_tile(turn_row_tile(raw_q[b], i), i, group)
                 cols = slice(i * OPERAND // ROW_TILES, (i + 1) * OPERAND // ROW_TILES)
                 nc.vector.tensor_tensor(out=squared[:, cols], in0=group[:, cols], in1=group[:, cols], op=ALU.mult)
+                if i % 2 == 1:
+                    keep_warm(1)
             return group, squared
 
         def turn_key_pair(raw, pair, g):
@@ -119,6 +127,7 @@ def tile_probcrossattention_pb_kernel(tc, q, k_mu, k_var, v_sample, out):
             for pair in range(ROW_TILES // 2):
                 for g in range(PASSES):
                     regroup_key_pair(turn_key_pair(raw, pair, g), pair, g, group)
+                keep_warm(1)
             return quantise_operand(group, label)
 
         def regroup_values(b, group, part):
@@ -244,9 +253,13 @@ def tile_probcrossattention_pb_kernel(tc, q, k_mu, k_var, v_sample, out):
         make_identity(nc, ident_f32[:])
         one = const.tile([P, 1], F32, name="one")
         nc.vector.memset(one[:], 1.0)
+        idle = const.tile([P, BANK], BF16, name="idle")
+        nc.vector.memset(idle[:], 0.0)
+        unread = spare.tile([P, BANK], F32, name="unread")
         nc.scalar.activation(out=one[:], in_=one[:], func=ACT.Sqrt)
 
         q_mx, qq_mx, k_mu_mx, k_var_mx = [], [], [], []
+        keep_warm(WARM_UP)
         for b in range(BATCH):
             q_group, squared = prepare_queries(b)
             q_mx.append(quantise_operand(q_group, "q%d" % b))

@@ -26,8 +26,9 @@ WORDS = OPERAND // PACK
 LOAD_PIECES = 2
 WARM_UP = 4
 VALUE_PARTS = 4
-VALUES_FROM = 1
-SHARED_FROM = 3
+GPSIMD_PARTS = 8
+VALUES_FROM = 2
+SHARED_FROM = 2
 
 ROWS_STATIONARY = "p (i g r u) -> p i g r u"
 
@@ -139,6 +140,19 @@ def tile_probcrossattention_pb_kernel(tc, q, k_mu, k_var, v_sample, out):
                 in_=raw_v[b][:]
                 .rearrange("p (t c) -> p t c", t=PACK)[:, :, part * width : (part + 1) * width]
                 .rearrange("p t (c i) -> p c t i", i=4),
+            )
+
+        def regroup_values_on_gpsimd(b, group, part):
+            width = CHANNELS // GPSIMD_PARTS
+            nc.gpsimd.tensor_scalar(
+                out=group[:, part * width * PACK : (part + 1) * width * PACK].rearrange("p (c t) -> p c t", t=PACK),
+                in0=raw_v[b][:]
+                .rearrange("p (t c) -> p t c", t=PACK)[:, :, part * width : (part + 1) * width]
+                .rearrange("p t c -> p c t"),
+                scalar1=1.0,
+                scalar2=0.0,
+                op0=ALU.mult,
+                op1=ALU.add,
             )
 
         def quantise_values(b, group, part):
@@ -270,18 +284,21 @@ def tile_probcrossattention_pb_kernel(tc, q, k_mu, k_var, v_sample, out):
         tiles = [(b, i) for b in range(BATCH) for i in range(ROW_TILES)]
         penalties = [penalty_tile(b, i) for (b, i) in tiles]
         v_mx = [new_packed(packed, "v%d" % b, CHANNELS) for b in range(BATCH)]
-        v_groups = [new_group() for b in range(BATCH)]
+        v_group = new_group()
         for part in range(VALUE_PARTS + 1):
             if part < VALUE_PARTS:
-                regroup_values(0, v_groups[0], part)
+                regroup_values(0, v_group, part)
             if part > 0:
-                quantise_values(0, v_groups[0], part - 1)
+                quantise_values(0, v_group, part - 1)
 
         def live(n):
             return 0 <= n < len(tiles)
 
         mean_sums, negs, lows, exps, e_turned, e_groups, e_mxs, products = {}, {}, {}, {}, {}, {}, {}, {}
         for step in range(-3, len(tiles) + 3):
+            if step < 8/1-3:
+                for j in range(1):
+                    regroup_values_on_gpsimd(1, v_group, GPSIMD_PARTS - 1 - (1 * (step + 3) + j))
             if live(step + 3):
                 b, i = tiles[step + 3]
                 mean_sums[step + 3] = channel_product(q_mx[b], k_mu_mx[b], i)
@@ -298,9 +315,7 @@ def tile_probcrossattention_pb_kernel(tc, q, k_mu, k_var, v_sample, out):
                 lows[step + 1] = row_minimum(negs[step + 1])
             if live(step - 3):
                 store_tile(step - 3, products[step - 3], e_mxs[step - 3][1])
-            if 0 <= step - VALUES_FROM < VALUE_PARTS:
-                regroup_values(1, v_groups[1], step - VALUES_FROM)
             if live(step - 1):
                 e_mxs[step - 1] = quantise_e(e_groups[step - 1], exps[step - 1][1])
-            if 0 <= step - VALUES_FROM - 1 < VALUE_PARTS:
-                quantise_values(1, v_groups[1], step - VALUES_FROM - 1)
+            if 0 <= step - VALUES_FROM < VALUE_PARTS:
+                quantise_values(1, v_group, VALUE_PARTS - 1 - (step - VALUES_FROM))

@@ -28,7 +28,7 @@ WARM_UP = 4
 VALUE_PARTS = 4
 GPSIMD_PARTS = 8
 VALUES_FROM = 2
-SHARED_FROM = 2
+SHARED_FROM = 3
 
 ROWS_STATIONARY = "p (i g r u) -> p i g r u"
 
@@ -54,6 +54,9 @@ def tile_probcrossattention_pb_kernel(tc, q, k_mu, k_var, v_sample, out):
         def keep_warm(count):
             for j in range(count):
                 nc.tensor.matmul(unread[:], idle[:, 0:P], idle[:], start=True, stop=True)
+
+        def keep_warm_behind(tile, width):
+            nc.tensor.matmul(unread[:, 0:width], ident_f32[:], tile[:, 0:width], start=True, stop=True)
 
         def load(x, b, label):
             raw = raws.tile([P, OPERAND], BF16, name="raw_%s%d" % (label, b))
@@ -253,7 +256,10 @@ def tile_probcrossattention_pb_kernel(tc, q, k_mu, k_var, v_sample, out):
                 nc.vector.tensor_scalar(
                     out=result[:, BANK:], in0=accs[1][:], scalar1=inv_sum[:], scalar2=None, op0=ALU.mult
                 )
-            nc.sync.dma_start(out=out[b].rearrange("(p i) c -> p i c", i=ROW_TILES)[:, i, :], in_=result[:])
+            rows = out[b].rearrange("(p i) c -> p i c", i=ROW_TILES)[:, i, :]
+            for h in range(HALVES):
+                cols = slice(h * BANK, (h + 1) * BANK)
+                nc.sync.dma_start(out=rows[:, cols], in_=result[:, cols])
 
         raw_q, raw_k_mu, raw_k_var, raw_v = [], [], [], []
         for b in range(BATCH):
@@ -302,8 +308,12 @@ def tile_probcrossattention_pb_kernel(tc, q, k_mu, k_var, v_sample, out):
             if live(step + 3):
                 b, i = tiles[step + 3]
                 mean_sums[step + 3] = channel_product(q_mx[b], k_mu_mx[b], i)
+            if step in (-1, 0):
+                keep_warm_behind(negs[step + 1], BANK // 2)
             if live(step - 2):
                 products[step - 2] = value_products(tiles[step - 2][0], e_mxs[step - 2][0])
+            if live(step - 3):
+                store_tile(step - 3, products[step - 3], e_mxs[step - 3][1])
             if live(step):
                 exps[step] = exp_tile(negs[step], lows[step])
                 e_turned[step] = turn_e(exps[step][0])
@@ -313,8 +323,6 @@ def tile_probcrossattention_pb_kernel(tc, q, k_mu, k_var, v_sample, out):
                 negs[step + 2] = negated_scores(mean_sums[step + 2], penalties[step + 2])
             if live(step + 1):
                 lows[step + 1] = row_minimum(negs[step + 1])
-            if live(step - 3):
-                store_tile(step - 3, products[step - 3], e_mxs[step - 3][1])
             if live(step - 1):
                 e_mxs[step - 1] = quantise_e(e_groups[step - 1], exps[step - 1][1])
             if 0 <= step - VALUES_FROM < VALUE_PARTS:

import math
from contextlib import ExitStack

import concourse.mybir as mybir
from concourse.masks import make_identity

F32 = mybir.dt.float32
BF16 = mybir.dt.bfloat16
U32 = mybir.dt.uint32
U8 = mybir.dt.uint8
FP8X4 = mybir.dt.float8_e4m3fn_x4
ACT = mybir.ActivationFunctionType
ALU = mybir.AluOpType
AXIS = mybir.AxisListType

P = 128
PACK = 4
BATCH, ROWS, CHANNELS = 2, 512, 1024
BETA = 2.35
ROW_TILES = ROWS // P
PASSES = CHANNELS // (P * PACK)
BANK = 512
HALVES = CHANNELS // BANK
OPERAND = ROWS * CHANNELS // P
WORDS = OPERAND // PACK
LOAD_PIECES = 2
WARM_UP = 4
VALUE_PARTS = 4
GPSIMD_PARTS = 8
VALUES_FROM = 2
SHARED_FROM = 3

ROWS_STATIONARY = "p (i g r u) -> p i g r u"

FLOPS = 3 * 2 * BATCH * ROWS * ROWS * CHANNELS


def tile_probcrossattention_pb_kernel(tc, q, k_mu, k_var, v_sample, out):
    nc = tc.nc
    with ExitStack() as ctx:
        const = ctx.enter_context(tc.tile_pool(name="const", bufs=1))
        raws = ctx.enter_context(tc.tile_pool(name="raws", bufs=1))
        groups = ctx.enter_context(tc.tile_pool(name="groups", bufs=5))
        packed = ctx.enter_context(tc.tile_pool(name="packed", bufs=1))
        per_tile = ctx.enter_context(tc.tile_pool(name="per_tile", bufs=BATCH * ROW_TILES))
        stream = ctx.enter_context(tc.tile_pool(name="stream", bufs=4))
        psum = ctx.enter_context(tc.psum_pool(name="psum", bufs=7))
        spare = ctx.enter_context(tc.psum_pool(name="spare", bufs=1))
        ctx.enter_context(tc.manual_schedule())

        def bank(dtype):
            return psum.tile([P, BANK], dtype, name="bank")

        def keep_warm(count):
            for j in range(count):
                nc.tensor.matmul(unread[:], idle[:, 0:P], idle[:], start=True, stop=True)

        def keep_warm_behind(tile, width):
            nc.tensor.matmul(unread[:, 0:width], ident_f32[:], tile[:, 0:width], start=True, stop=True)

        def load(x, b, label):
            raw = raws.tile([P, OPERAND], BF16, name="raw_%s%d" % (label, b))
            rows = x[b].rearrange("(p i) c -> p (i c)", i=ROW_TILES)
            piece = OPERAND // LOAD_PIECES
            for j in range(LOAD_PIECES):
                nc.sync.dma_start(out=raw[:, j * piece : (j + 1) * piece], in_=rows[:, j * piece : (j + 1) * piece])
            return raw

        def new_group():
            return groups.tile([P, OPERAND], BF16, name="group", align_bytes=64)

        def new_packed(pool, label, width):
            return (
                pool.tile([P, width], U32, name="codes_" + label, align_bytes=64),
                pool.tile([P, width], U8, name="scales_" + label, align_bytes=64),
            )

        def quantise(mx, group, first, width):
            nc.vector.quantize_mx(
                out=mx[0][:, first : first + width].bitcast(FP8X4),
                scales=mx[1][:, first : first + width],
                in_=group[:, first * PACK : (first + width) * PACK],
            )

        def quantise_operand(group, label):
            mx = new_packed(packed, label, WORDS)
            quantise(mx, group, 0, WORDS)
            return mx

        def turn_row_tile(raw, i):
            words = raw[:].bitcast(F32)
            turned = bank(F32)
            for w in range(BANK // P):
                first = i * BANK + w * P
                nc.tensor.transpose(turned[:, w * P : (w + 1) * P], words[:, first : first + P], ident_f32[:])
            return turned

        def regroup_row_tile(turned, i, group):
            nc.scalar.copy(
                out=group[:].bitcast(F32).rearrange(ROWS_STATIONARY, i=ROW_TILES, g=PASSES, u=2)[:, i],
                in_=turned[:].rearrange("p (g u r) -> p g r u", g=PASSES, u=2),
            )

        def prepare_queries(b):
            group, squared = new_group(), new_group()
            for i in range(ROW_TILES):
                regroup_row_tile(turn_row_tile(raw_q[b], i), i, group)
                cols = slice(i * OPERAND // ROW_TILES, (i + 1) * OPERAND // ROW_TILES)
                nc.vector.tensor_tensor(out=squared[:, cols], in0=group[:, cols], in1=group[:, cols], op=ALU.mult)
                if i % 2 == 1:
                    keep_warm(1)
            return group, squared

        def turn_key_pair(raw, pair, g):
            words = raw[:].bitcast(F32)
            turned = bank(F32)
            for x in range(BANK // P):
                first = (2 * pair + x // 2) * BANK + (2 * g + x % 2) * P
                nc.tensor.transpose(turned[:, x * P : (x + 1) * P], words[:, first : first + P], ident_f32[:])
            return turned

        def regroup_key_pair(turned, pair, g, group):
            first = (g * 2 + pair) * BANK
            nc.scalar.copy(
                out=group[:].bitcast(F32)[:, first : first + BANK].rearrange("p (r x) -> p r x", x=4),
                in_=turned[:].rearrange("p (x r) -> p r x", x=4),
            )

        def prepare_keys(raw, label):
            group = new_group()
            for pair in range(ROW_TILES // 2):
                for g in range(PASSES):
                    regroup_key_pair(turn_key_pair(raw, pair, g), pair, g, group)
                keep_warm(1)
            return quantise_operand(group, label)

        def regroup_values(b, group, part):
            width = CHANNELS // VALUE_PARTS
            nc.vector.tensor_copy(
                out=group[:, part * width * PACK : (part + 1) * width * PACK].rearrange(
                    "p (c i t) -> p c t i", i=4, t=PACK
                ),
                in_=raw_v[b][:]
                .rearrange("p (t c) -> p t c", t=PACK)[:, :, part * width : (part + 1) * width]
                .rearrange("p t (c i) -> p c t i", i=4),
            )

        def regroup_values_on_gpsimd(b, group, part):
            width = CHANNELS // GPSIMD_PARTS
            nc.gpsimd.tensor_scalar(
                out=group[:, part * width * PACK : (part + 1) * width * PACK].rearrange("p (c t) -> p c t", t=PACK),
                in0=raw_v[b][:]
                .rearrange("p (t c) -> p t c", t=PACK)[:, :, part * width : (part + 1) * width]
                .rearrange("p t c -> p c t"),
                scalar1=1.0,
                scalar2=0.0,
                op0=ALU.mult,
                op1=ALU.add,
            )

        def quantise_values(b, group, part):
            quantise(v_mx[b], group, part * CHANNELS // VALUE_PARTS, CHANNELS // VALUE_PARTS)

        def channel_product(rows_mx, keys_mx, i):
            acc = bank(F32)
            for g in range(PASSES):
                rows = slice((i * PASSES + g) * P, (i * PASSES + g + 1) * P)
                keys = slice(g * ROWS, (g + 1) * ROWS)
                nc.tensor.matmul_mx(
                    out=acc[:],
                    lhsT=rows_mx[0][:, rows].bitcast(FP8X4),
                    lhsT_scale=rows_mx[1][:, rows],
                    rhs=keys_mx[0][:, keys].bitcast(FP8X4),
                    rhs_scale=keys_mx[1][:, keys],
                    start=(g == 0),
                    stop=(g == PASSES - 1),
                )
            return acc

        def penalty_tile(b, i):
            var_sum = channel_product(qq_mx[b], k_var_mx[b], i)
            penalty = per_tile.tile([P, ROWS], F32, name="penalty")
            nc.scalar.activation(out=penalty[:], in_=var_sum[:], func=ACT.Sqrt, scale=BETA * BETA / CHANNELS)
            return penalty

        def negated_scores(mean_sum, penalty):
            neg = stream.tile([P, ROWS], F32, name="neg")
            nc.vector.scalar_tensor_tensor(
                out=neg[:],
                in0=mean_sum[:],
                scalar=-1.0 / math.sqrt(CHANNELS),
                in1=penalty[:],
                op0=ALU.mult,
                op1=ALU.add,
            )
            return neg

        def row_minimum(neg):
            low = stream.tile([P, 1], F32, name="low")
            nc.vector.tensor_reduce(out=low[:], in_=neg[:], axis=AXIS.X, op=ALU.min)
            return low

        def exp_tile(neg, low):
            e = stream.tile([P, ROWS], BF16, name="e")
            row_sum = stream.tile([P, 1], F32, name="row_sum")
            nc.scalar.activation(
                out=e[:], in_=neg[:], func=ACT.Exp, scale=-1.0, bias=low[:], accum_out=row_sum[:]
            )
            return e, row_sum

        def turn_e(e):
            words = e[:].bitcast(F32)
            turned = bank(F32)
            for u in range(2):
                nc.tensor.transpose(turned[:, u * P : (u + 1) * P], words[:, u * P : (u + 1) * P], ident_f32[:])
            return turned

        def regroup_e(turned):
            e_group = stream.tile([P, ROWS], BF16, name="e_group", align_bytes=64)
            nc.scalar.copy(
                out=e_group[:].bitcast(F32).rearrange("p (r u) -> p r u", u=2),
                in_=turned[:, 0 : 2 * P].rearrange("p (u r) -> p r u", u=2),
            )
            return e_group

        def quantise_e(e_group, row_sum):
            inv_sum = stream.tile([P, 1], F32, name="inv_sum")
            nc.vector.reciprocal(out=inv_sum[:], in_=row_sum[:])
            e_mx = new_packed(stream, "e", P)
            quantise(e_mx, e_group, 0, P)
            return e_mx, inv_sum

        def value_products(b, e_mx):
            accs = []
            for h in range(HALVES):
                cols = slice(h * BANK, (h + 1) * BANK)
                accs.append(bank(F32))
                nc.tensor.matmul_mx(
                    out=accs[h][:],
                    lhsT=e_mx[0][:].bitcast(FP8X4),
                    lhsT_scale=e_mx[1][:],
                    rhs=v_mx[b][0][:, cols].bitcast(FP8X4),
                    rhs_scale=v_mx[b][1][:, cols],
                    start=True,
                    stop=True,
                )
            return accs

        def store_tile(n, accs, inv_sum):
            b, i = tiles[n]
            result = stream.tile([P, CHANNELS], F32, name="result")
            nc.scalar.activation(out=result[:, 0:BANK], in_=accs[0][:], func=ACT.Copy, scale=inv_sum[:])
            if n < SHARED_FROM:
                nc.scalar.activation(out=result[:, BANK:], in_=accs[1][:], func=ACT.Copy, scale=inv_sum[:])
            else:
                nc.vector.tensor_scalar(
                    out=result[:, BANK:], in0=accs[1][:], scalar1=inv_sum[:], scalar2=None, op0=ALU.mult
                )
            rows = out[b].rearrange("(p i) c -> p i c", i=ROW_TILES)[:, i, :]
            for h in range(HALVES):
                cols = slice(h * BANK, (h + 1) * BANK)
                nc.sync.dma_start(out=rows[:, cols], in_=result[:, cols])

        raw_q, raw_k_mu, raw_k_var, raw_v = [], [], [], []
        for b in range(BATCH):
            raw_q.append(load(q, b, "q"))
            raw_k_var.append(load(k_var, b, "k_var"))
            raw_k_mu.append(load(k_mu, b, "k_mu"))
        for b in range(BATCH):
            raw_v.append(load(v_sample, b, "v"))

        ident_f32 = const.tile([P, P], F32, name="ident_f32")
        make_identity(nc, ident_f32[:])
        one = const.tile([P, 1], F32, name="one")
        nc.vector.memset(one[:], 1.0)
        idle = const.tile([P, BANK], BF16, name="idle")
        nc.vector.memset(idle[:], 0.0)
        unread = spare.tile([P, BANK], F32, name="unread")
        nc.scalar.activation(out=one[:], in_=one[:], func=ACT.Sqrt)

        q_mx, qq_mx, k_mu_mx, k_var_mx = [], [], [], []
        keep_warm(WARM_UP)
        for b in range(BATCH):
            q_group, squared = prepare_queries(b)
            q_mx.append(quantise_operand(q_group, "q%d" % b))
            qq_mx.append(quantise_operand(squared, "qq%d" % b))
            k_var_mx.append(prepare_keys(raw_k_var[b], "k_var%d" % b))
            k_mu_mx.append(prepare_keys(raw_k_mu[b], "k_mu%d" % b))

        tiles = [(b, i) for b in range(BATCH) for i in range(ROW_TILES)]
        penalties = [penalty_tile(b, i) for (b, i) in tiles]
        v_mx = [new_packed(packed, "v%d" % b, CHANNELS) for b in range(BATCH)]
        v_group = new_group()
        for part in range(VALUE_PARTS + 1):
            if part < VALUE_PARTS:
                regroup_values(0, v_group, part)
            if part > 0:
                quantise_values(0, v_group, part - 1)

        def live(n):
            return 0 <= n < len(tiles)

        mean_sums, negs, lows, exps, e_turned, e_groups, e_mxs, products = {}, {}, {}, {}, {}, {}, {}, {}
        for step in range(-3, len(tiles) + 3):
            if step < 8/1-3:
                for j in range(1):
                    regroup_values_on_gpsimd(1, v_group, GPSIMD_PARTS - 1 - (1 * (step + 3) + j))
            if live(step + 3):
                b, i = tiles[step + 3]
                mean_sums[step + 3] = channel_product(q_mx[b], k_mu_mx[b], i)
            if step in (-1, 0):
                keep_warm_behind(negs[step + 1], BANK // 2)
            if live(step - 2):
                products[step - 2] = value_products(tiles[step - 2][0], e_mxs[step - 2][0])
            if live(step - 3):
                store_tile(step - 3, products[step - 3], e_mxs[step - 3][1])
            if live(step):
                exps[step] = exp_tile(negs[step], lows[step])
                e_turned[step] = turn_e(exps[step][0])
            if live(step - 1):
                e_groups[step - 1] = regroup_e(e_turned[step - 1])
            if live(step + 2):
                negs[step + 2] = negated_scores(mean_sums[step + 2], penalties[step + 2])
            if live(step + 1):
                lows[step + 1] = row_minimum(negs[step + 1])
            if live(step - 1):
                e_mxs[step - 1] = quantise_e(e_groups[step - 1], exps[step - 1][1])
            if 0 <= step - VALUES_FROM < VALUE_PARTS:
                quantise_values(1, v_group, VALUE_PARTS - 1 - (step - VALUES_FROM))
